import numpy as np
import ml_dtypes


def mxq(x, axis, fmt="e4m3"):
    dtype, down = {"e4m3": (ml_dtypes.float8_e4m3fn, 7), "e5m2": (ml_dtypes.float8_e5m2, 14)}[fmt]
    v = np.moveaxis(np.asarray(x, np.float32).astype(ml_dtypes.bfloat16).astype(np.float64), axis, -1)
    blocks = v.reshape(v.shape[:-1] + (-1, 32))
    amax = np.abs(blocks).max(-1, keepdims=True)
    byte = np.maximum(np.where(amax > 0, np.frexp(amax)[1] - 1 + 127, 0) - down, 1)
    scale = np.exp2(byte - 127.0)
    codes = (blocks / scale).astype(np.float32).astype(dtype).astype(np.float64)
    return np.moveaxis((codes * scale).reshape(v.shape), -1, axis)


WIDE = False


def mx_kscale(k):
    if not WIDE:
        return np.ones(k)
    levels = np.array([10, -10, 5, -5, 0])
    a = np.random.permutation(np.resize(levels, k // 512 * 4)).reshape(k // 512, 4)
    idx = np.arange(k)
    return np.exp2(a[idx // 512, idx % 128 // 32])


BF16 = ml_dtypes.bfloat16


def bf(x):
    return np.asarray(x, np.float32).astype(BF16)


def f64(x):
    return np.asarray(x).astype(np.float64)


T, DIM, NH, NKV = 512, 2048, 16, 4
HD = DIM // NH
REP = NH // NKV
V_MEAN, V_STD = 0.75, 0.65


def setup_inputs():
    t = mx_kscale(NKV * HD).reshape(NKV, HD)
    tw = np.repeat(t, REP, axis=0).reshape(NH * HD, 1)
    return {"q": bf(np.random.standard_normal((NH, T, HD))),
            "k": bf(np.random.standard_normal((NKV, T, HD))),
            "v": bf((V_MEAN + V_STD * np.random.standard_normal((NKV, T, HD))) * t[:, None, :]),
            "W_o": bf(np.random.standard_normal((NH * HD, DIM)) * 2.0 / np.sqrt(NH * HD) / tw)}


def reference(q, k, v, W_o):
    qg = f64(q).reshape(NKV, REP * T, HD)
    s = qg @ f64(k).transpose(0, 2, 1) / np.sqrt(HD)
    causal = np.arange(T)[:, None] >= np.arange(T)[None, :]
    s = np.where(causal, s.reshape(NKV, REP, T, T), -np.inf).reshape(NKV, REP * T, T)
    e = np.exp(s - s.max(-1, keepdims=True))
    o = (mxq(e, 2, "e4m3") @ mxq(f64(v), 1, "e4m3")) / e.sum(-1, keepdims=True)
    a = o.reshape(NH, T, HD).transpose(1, 0, 2).reshape(T, NH * HD)
    return mxq(a, 1, "e4m3") @ mxq(f64(W_o), 0, "e4m3")

@@ -1,0 +1,390 @@
+import math
+from contextlib import ExitStack
+
+import concourse.mybir as mybir
+from concourse.masks import make_identity
+
+F32 = mybir.dt.float32
+BF16 = mybir.dt.bfloat16
+U32 = mybir.dt.uint32
+U8 = mybir.dt.uint8
+FP8X4 = mybir.dt.float8_e4m3fn_x4
+ALU = mybir.AluOpType
+ACT = mybir.ActivationFunctionType
+AXIS = mybir.AxisListType
+
+P = 128
+T = 512
+HEADS = 16
+GROUPS = 4
+REP = HEADS // GROUPS
+HD = 128
+DIM = HEADS * HD
+BLOCKS = T // P
+PACK = 4
+K_PASS = P * PACK
+PASSES = DIM // K_PASS
+N_TILE = 512
+COLUMN_BLOCKS = DIM // N_TILE
+PIECES = COLUMN_BLOCKS * PASSES
+SCALE = 1.0 / math.sqrt(HD)
+MASK_VALUE = -3.0e38
+E_BUFFERS = 2
+WEIGHTS_START = 13
+
+FLOPS = 2 * (2 * HEADS * T * T * HD) + 2 * T * DIM * DIM
+
+
+def tile_fusedselfattention_pa_kernel(tc, q, k, v, W_o, out):
+    nc = tc.nc
+    units = [(block, group) for block in reversed(range(BLOCKS)) for group in range(GROUPS)]
+    n_units = len(units)
+    blocks_in_order = [units[i * GROUPS][0] for i in range(BLOCKS)]
+    held = {}
+
+    with ExitStack() as sbuf:
+        sbuf.enter_context(tc.manual_schedule())
+        keep = sbuf.enter_context(tc.tile_pool(name="keep", bufs=1))
+        stats = sbuf.enter_context(tc.tile_pool(name="stats", bufs=3))
+        stage = sbuf.enter_context(tc.tile_pool(name="stage", bufs=2))
+        weights_stage = sbuf.enter_context(tc.tile_pool(name="weights_stage", bufs=4))
+        results = sbuf.enter_context(tc.tile_pool(name="results", bufs=BLOCKS))
+
+        identity_bf16 = keep.tile([P, P], BF16)
+        identity_f32 = keep.tile([P, P], F32)
+        causal_f32 = keep.tile([P, P], F32)
+        causal_mask = keep.tile([P, P], BF16)
+        warm = keep.tile([P, 1], F32)
+        k_rows = keep.tile([P, GROUPS * BLOCKS, HD], BF16)
+        k_t = keep.tile([P, GROUPS, T], BF16)
+        q_rows = [keep.tile([P, HEADS, HD], BF16, name="q_rows%d" % b) for b in range(BLOCKS)]
+        q_t = [keep.tile([P, HEADS, P], BF16, name="q_t%d" % b) for b in range(BLOCKS)]
+        v_rows = keep.tile([P, GROUPS * PACK, HD], BF16)
+        v_grouped = keep.tile([P, GROUPS * HD * PACK], BF16, align_bytes=64)
+        v_codes = keep.tile([P, GROUPS * HD], U32, align_bytes=64)
+        v_scales = keep.tile([P, GROUPS * HD], U8, align_bytes=64)
+        w_rows = [keep.tile([P, PASSES * PACK, N_TILE], BF16, name="w_rows%d" % n) for n in range(COLUMN_BLOCKS)]
+        w_codes = keep.tile([P, COLUMN_BLOCKS, PASSES, N_TILE], U32, align_bytes=64)
+        w_scales = keep.tile([P, COLUMN_BLOCKS, PASSES, N_TILE], U8, align_bytes=64)
+        a_codes = keep.tile([P, BLOCKS, PASSES, P], U32, align_bytes=64)
+        a_scales = keep.tile([P, BLOCKS, PASSES, P], U8, align_bytes=64)
+        e_rows = [keep.tile([P, REP, T], BF16, name="e_rows%d" % b) for b in range(E_BUFFERS)]
+
+        def load_keys(group):
+            nc.sync.dma_start(
+                out=k_rows[:, group * BLOCKS : (group + 1) * BLOCKS, :],
+                in_=k[group, :, :].rearrange("(b p) d -> p b d", p=P),
+            )
+
+        def load_queries(unit):
+            block, group = units[unit]
+            heads = slice(group * REP, (group + 1) * REP)
+            nc.sync.dma_start(
+                out=q_rows[block][:, heads, :],
+                in_=q[heads, block * P : (block + 1) * P, :].rearrange("h p d -> p h d"),
+            )
+
+        def load_weights(n):
+            columns = W_o[:, n * N_TILE : (n + 1) * N_TILE].rearrange("(cu p e) n -> p cu e n", p=P, e=2)
+            rows = w_rows[n][:].rearrange("p (cu e) n -> p cu e n", e=2)
+            for e in range(2):
+                nc.sync.dma_start(out=rows[:, :, e, :], in_=columns[:, :, e, :])
+
+        for group in range(GROUPS):
+            load_keys(group)
+            load_queries(group)
+        nc.sync.dma_start(
+            out=v_rows[:].rearrange("p (gu e) d -> p gu (e d)", e=2),
+            in_=v.rearrange("g (u p e) d -> p (g u) (e d)", u=2, p=P, e=2),
+        )
+        for unit in range(GROUPS, n_units):
+            load_queries(unit)
+        for n in range(COLUMN_BLOCKS):
+            load_weights(n)
+
+        nc.vector.memset(warm[:], 0.0)
+        nc.scalar.activation(out=warm[:], in_=warm[:], func=ACT.Exp)
+        make_identity(nc, identity_bf16[:])
+        make_identity(nc, identity_f32[:])
+        nc.gpsimd.memset(causal_f32[:], 0.0)
+        nc.gpsimd.affine_select(
+            out=causal_f32[:],
+            in_=causal_f32[:],
+            pattern=[[-1, P]],
+            compare_op=ALU.is_ge,
+            fill=MASK_VALUE,
+            base=0,
+            channel_multiplier=1,
+        )
+        nc.vector.tensor_copy(out=causal_mask[:], in_=causal_f32[:])
+
+        nc.gpsimd.tensor_scalar(
+            out=v_grouped[:].rearrange("p (g d t) -> p g d t", g=GROUPS, t=PACK),
+            in0=v_rows[:].rearrange("p (g t) d -> p g d t", t=PACK),
+            scalar1=1.0,
+            scalar2=0.0,
+            op0=ALU.mult,
+            op1=ALU.add,
+        )
+
+        def quantise_values():
+            nc.vector.quantize_mx(out=v_codes[:].bitcast(FP8X4), scales=v_scales[:], in_=v_grouped[:])
+
+        def regroup_weights(piece):
+            n, c = divmod(piece, PASSES)
+            rows = w_rows[n][:, c * PACK : (c + 1) * PACK, :]
+            w_grouped = weights_stage.tile([P, N_TILE * PACK], BF16, align_bytes=64)
+            grouped_runs = w_grouped[:].rearrange("p (m i t) -> p m t i", i=4, t=PACK)
+            row_runs = rows.rearrange("p t (m i) -> p m t i", i=4)
+            if c < 2 or (c == 2 and n % 2 == 0):
+                nc.vector.tensor_copy(out=grouped_runs, in_=row_runs)
+            else:
+                nc.scalar.copy(out=grouped_runs, in_=row_runs)
+            held[("w_grouped", piece)] = w_grouped
+
+        def quantise_weights(piece):
+            n, c = divmod(piece, PASSES)
+            nc.vector.quantize_mx(
+                out=w_codes[:, n, c, :].bitcast(FP8X4),
+                scales=w_scales[:, n, c, :],
+                in_=held[("w_grouped", piece)][:],
+            )
+
+        with ExitStack() as psum:
+            score_banks = psum.enter_context(tc.psum_pool(name="score_banks", bufs=4))
+            other_banks = psum.enter_context(tc.psum_pool(name="other_banks", bufs=4))
+
+            def transpose_keys(group):
+                bank = other_banks.tile([P, BLOCKS, P], BF16, tag="bank")
+                for b in range(BLOCKS):
+                    nc.tensor.transpose(bank[:, b, :], k_rows[:, group * BLOCKS + b, :], identity_bf16[:])
+                nc.scalar.copy(out=k_t[:, group, :], in_=bank[:].rearrange("p b j -> p (b j)"))
+
+            def transpose_queries(unit):
+                block, group = units[unit]
+                bank = other_banks.tile([P, REP, P], BF16, tag="bank")
+                for r in range(REP):
+                    nc.tensor.transpose(bank[:, r, :], q_rows[block][:, group * REP + r, :], identity_bf16[:])
+                nc.vector.tensor_copy(out=q_t[block][:, group * REP : (group + 1) * REP, :], in_=bank[:])
+
+            def scores_and_row_maxima(unit, pair):
+                block, group = units[unit]
+                keys = (block + 1) * P
+                diagonal = slice(block * P, keys)
+                if pair == 0 and block < BLOCKS - 1 and group < E_BUFFERS:
+                    nc.vector.memset(e_rows[unit % E_BUFFERS][:, :, keys : keys + P], 0.0)
+                row_max = stats.tile([P, 2], F32)
+                banks = []
+                for r in range(2):
+                    queries = q_t[block][:, group * REP + 2 * pair + r, :]
+                    scores = score_banks.tile([P, T], F32, tag="bank")
+                    if block > 0:
+                        nc.tensor.matmul(
+                            scores[:, 0 : block * P],
+                            lhsT=queries,
+                            rhs=k_t[:, group, 0 : block * P],
+                            start=True,
+                            stop=True,
+                        )
+                    nc.tensor.matmul(
+                        scores[:, diagonal], lhsT=queries, rhs=k_t[:, group, diagonal], start=True, stop=False
+                    )
+                    nc.tensor.matmul(
+                        scores[:, diagonal], lhsT=identity_bf16[:], rhs=causal_mask[:], start=False, stop=True
+                    )
+                    nc.vector.tensor_reduce(
+                        out=row_max[:, r : r + 1], in_=scores[:, 0:keys], axis=AXIS.X, op=ALU.max
+                    )
+                    banks.append(scores)
+                held[("scores", unit, pair)] = banks
+                held[("row_max", unit, pair)] = row_max
+
+            def exponent_biases(unit, pair):
+                bias = stats.tile([P, 2], F32)
+                nc.vector.tensor_scalar_mul(out=bias[:], in0=held[("row_max", unit, pair)][:], scalar1=-SCALE)
+                held[("bias", unit, pair)] = bias
+
+            def exponentials(unit, pair):
+                block, group = units[unit]
+                keys = (block + 1) * P
+                if pair == 0:
+                    row_sum = stats.tile([P, REP], F32)
+                    held[("row_sum", unit)] = row_sum
+                for r in range(2):
+                    head = 2 * pair + r
+                    nc.scalar.activation(
+                        out=e_rows[unit % E_BUFFERS][:, head, 0:keys],
+                        in_=held[("scores", unit, pair)][r][:, 0:keys],
+                        func=ACT.Exp,
+                        bias=held[("bias", unit, pair)][:, r : r + 1],
+                        scale=SCALE,
+                        accum_out=held[("row_sum", unit)][:, head : head + 1],
+                    )
+
+            def transpose_exponentials(unit, pair):
+                bank = other_banks.tile([P, 2, 2 * P], F32, tag="bank")
+                for r in range(2):
+                    words = e_rows[unit % E_BUFFERS][:, 2 * pair + r, :].bitcast(F32)
+                    for u in range(2):
+                        nc.tensor.transpose(
+                            bank[:, u, r * P : (r + 1) * P], words[:, u * P : (u + 1) * P], identity_f32[:]
+                        )
+                held[("e_bank", unit, pair)] = bank
+
+            def copy_exponentials(unit, pair):
+                if pair == 0:
+                    e_grouped = stage.tile([P, REP * P * PACK], BF16, align_bytes=64)
+                    held[("e_grouped", unit)] = e_grouped
+                grouped_words = held[("e_grouped", unit)][:].bitcast(F32).rearrange("p (x u) -> p x u", u=2)
+                nc.scalar.copy(
+                    out=grouped_words[:, pair * 2 * P : (pair + 1) * 2 * P, :],
+                    in_=held[("e_bank", unit, pair)][:].rearrange("p u x -> p x u"),
+                )
+
+            def quantise_exponentials(unit):
+                e_codes = stage.tile([P, REP * P], U32, align_bytes=64)
+                e_scales = stage.tile([P, REP * P], U8, align_bytes=64)
+                nc.vector.quantize_mx(
+                    out=e_codes[:].bitcast(FP8X4), scales=e_scales[:], in_=held[("e_grouped", unit)][:]
+                )
+                held[("e_codes", unit)] = (e_codes, e_scales)
+
+            def weighted_values(unit):
+                block, group = units[unit]
+                e_codes, e_scales = held[("e_codes", unit)]
+                o_bank = other_banks.tile([P, REP, HD], F32, tag="bank")
+                for r in range(REP):
+                    nc.tensor.matmul_mx(
+                        out=o_bank[:, r, :],
+                        lhsT=e_codes[:, r * P : (r + 1) * P].bitcast(FP8X4),
+                        lhsT_scale=e_scales[:, r * P : (r + 1) * P],
+                        rhs=v_codes[:, group * HD : (group + 1) * HD].bitcast(FP8X4),
+                        rhs_scale=v_scales[:, group * HD : (group + 1) * HD],
+                        start=True,
+                        stop=True,
+                    )
+                held[("o_bank", unit)] = o_bank
+
+            def invert_row_sums(unit):
+                inverse_sum = stats.tile([P, REP], F32)
+                nc.vector.reciprocal(out=inverse_sum[:], in_=held[("row_sum", unit)][:])
+                held[("inverse_sum", unit)] = inverse_sum
+
+            def divide_by_row_sums(unit):
+                a_rows = stage.tile([P, REP * HD], BF16)
+                nc.vector.tensor_tensor(
+                    out=a_rows[:].rearrange("p (r d) -> p r d", r=REP),
+                    in0=held[("o_bank", unit)][:],
+                    in1=held[("inverse_sum", unit)][:].unsqueeze(2).to_broadcast([P, REP, HD]),
+                    op=ALU.mult,
+                )
+                held[("a_rows", unit)] = a_rows
+
+            def transpose_attention(unit):
+                words = held[("a_rows", unit)][:].bitcast(F32)
+                bank = other_banks.tile([P, 2, P], F32, tag="bank")
+                for u in range(2):
+                    nc.tensor.transpose(bank[:, u, :], words[:, u * P : (u + 1) * P], identity_f32[:])
+                held[("a_bank", unit)] = bank
+
+            def copy_attention(unit):
+                a_grouped = stage.tile([P, P * PACK], BF16, align_bytes=64)
+                nc.scalar.copy(
+                    out=a_grouped[:].bitcast(F32).rearrange("p (i u) -> p i u", u=2),
+                    in_=held[("a_bank", unit)][:].rearrange("p u i -> p i u"),
+                )
+                held[("a_grouped", unit)] = a_grouped
+
+            def quantise_attention(unit):
+                block, group = units[unit]
+                nc.vector.quantize_mx(
+                    out=a_codes[:, block, group, :].bitcast(FP8X4),
+                    scales=a_scales[:, block, group, :],
+                    in_=held[("a_grouped", unit)][:],
+                )
+
+            def project_piece(piece):
+                n, c = divmod(piece, PASSES)
+                if c == 0:
+                    banks = score_banks if n % 2 == 0 else other_banks
+                    sums = []
+                    for block in blocks_in_order:
+                        block_sum = banks.tile([P, N_TILE], F32, tag="bank")
+                        sums.append(block_sum)
+                    held[("sums", n)] = sums
+                for i, block in enumerate(blocks_in_order):
+                    nc.tensor.matmul_mx(
+                        out=held[("sums", n)][i][:],
+                        lhsT=a_codes[:, block, c, :].bitcast(FP8X4),
+                        lhsT_scale=a_scales[:, block, c, :],
+                        rhs=w_codes[:, n, c, :].bitcast(FP8X4),
+                        rhs_scale=w_scales[:, n, c, :],
+                        start=(c == 0),
+                        stop=(c == PASSES - 1),
+                    )
+
+            def store_column_block(n):
+                for i, block in enumerate(blocks_in_order):
+                    result = results.tile([P, N_TILE], F32)
+                    if i < BLOCKS - 1:
+                        nc.scalar.copy(out=result[:], in_=held[("sums", n)][i][:])
+                    else:
+                        nc.vector.tensor_copy(out=result[:], in_=held[("sums", n)][i][:])
+                    nc.sync.dma_start(
+                        out=out[block * P : (block + 1) * P, n * N_TILE : (n + 1) * N_TILE], in_=result[:]
+                    )
+
+            def is_unit(unit):
+                return 0 <= unit < n_units
+
+            def is_piece(piece):
+                return 0 <= piece < PIECES
+
+            for s in range(-3, WEIGHTS_START + PIECES + 7):
+                w = s - WEIGHTS_START
+                if is_unit(s + 1):
+                    scores_and_row_maxima(s + 1, 0)
+                if is_unit(s):
+                    transpose_exponentials(s, 0)
+                    transpose_exponentials(s, 1)
+                if is_unit(s - 3):
+                    copy_attention(s - 3)
+                if is_unit(s):
+                    copy_exponentials(s, 0)
+                if is_piece(w - 7) and (w - 7) % PASSES == PASSES - 1:
+                    store_column_block((w - 7) // PASSES)
+                if is_piece(w - 4):
+                    project_piece(w - 4)
+                if s == 0:
+                    quantise_values()
+                if is_unit(s + 1):
+                    exponent_biases(s + 1, 0)
+                    scores_and_row_maxima(s + 1, 1)
+                if is_unit(s - 1):
+                    weighted_values(s - 1)
+                if is_unit(s):
+                    copy_exponentials(s, 1)
+                if is_unit(s - 3):
+                    quantise_attention(s - 3)
+                if is_unit(s - 2):
+                    transpose_attention(s - 2)
+                if is_unit(s + 1):
+                    exponentials(s + 1, 0)
+                if is_unit(s):
+                    invert_row_sums(s)
+                if is_unit(s + 1):
+                    exponent_biases(s + 1, 1)
+                if is_unit(s - 1):
+                    divide_by_row_sums(s - 1)
+                if is_unit(s):
+                    quantise_exponentials(s)
+                if is_piece(w):
+                    regroup_weights(w)
+                if is_unit(s + 1):
+                    exponentials(s + 1, 1)
+                if is_unit(s + 3):
+                    if s + 3 < GROUPS:
+                        transpose_keys(s + 3)
+                    transpose_queries(s + 3)
+                if is_piece(w - 1):
+                    quantise_weights(w - 1)

@@ -48,7 +48,7 @@ def tile_fusedselfattention_pa_kernel(tc, q, k, v, W_o, out):
         stats = sbuf.enter_context(tc.tile_pool(name="stats", bufs=3))
         stage = sbuf.enter_context(tc.tile_pool(name="stage", bufs=2))
         weights_stage = sbuf.enter_context(tc.tile_pool(name="weights_stage", bufs=4))
-        results = sbuf.enter_context(tc.tile_pool(name="results", bufs=BLOCKS))
+        results = sbuf.enter_context(tc.tile_pool(name="results", bufs=2 * BLOCKS))
 
         identity_bf16 = keep.tile([P, P], BF16)
         identity_f32 = keep.tile([P, P], F32)
@@ -170,14 +170,17 @@ def tile_fusedselfattention_pa_kernel(tc, q, k, v, W_o, out):
             def scores_and_row_maxima(unit, pair):
                 block, group = units[unit]
                 keys = (block + 1) * P
+                per_bank = 1 if block > 1 else 2
                 diagonal = slice(block * P, keys)
                 if pair == 0 and block < BLOCKS - 1 and group < E_BUFFERS:
-                    nc.vector.memset(e_rows[unit % E_BUFFERS][:, :, keys : keys + P], 0.0)
+                    nc.gpsimd.memset(e_rows[unit % E_BUFFERS][:, :, keys : keys + P], 0.0)
                 row_max = stats.tile([P, 2], F32)
                 banks = []
                 for r in range(2):
                     queries = q_t[block][:, group * REP + 2 * pair + r, :]
-                    scores = score_banks.tile([P, T], F32, tag="bank")
+                    if r % per_bank == 0:
+                        bank = score_banks.tile([P, per_bank, T // per_bank], F32, tag="bank")
+                    scores = bank[:, r % per_bank, 0:keys]
                     if block > 0:
                         nc.tensor.matmul(
                             scores[:, 0 : block * P],
@@ -192,16 +195,17 @@ def tile_fusedselfattention_pa_kernel(tc, q, k, v, W_o, out):
                     nc.tensor.matmul(
                         scores[:, diagonal], lhsT=identity_bf16[:], rhs=causal_mask[:], start=False, stop=True
                     )
-                    nc.vector.tensor_reduce(
-                        out=row_max[:, r : r + 1], in_=scores[:, 0:keys], axis=AXIS.X, op=ALU.max
-                    )
+                    if r % per_bank == per_bank - 1:
+                        nc.vector.tensor_reduce(
+                            out=row_max[:, r + 1 - per_bank : r + 1], in_=bank[:, :, 0:keys], axis=AXIS.X, op=ALU.max
+                        )
                     banks.append(scores)
                 held[("scores", unit, pair)] = banks
                 held[("row_max", unit, pair)] = row_max
 
             def exponent_biases(unit, pair):
                 bias = stats.tile([P, 2], F32)
-                nc.vector.tensor_scalar_mul(out=bias[:], in0=held[("row_max", unit, pair)][:], scalar1=-SCALE)
+                nc.scalar.activation(out=bias[:], in_=held[("row_max", unit, pair)][:], func=ACT.Copy, scale=-SCALE)
                 held[("bias", unit, pair)] = bias
 
             def exponentials(unit, pair):
@@ -214,7 +218,7 @@ def tile_fusedselfattention_pa_kernel(tc, q, k, v, W_o, out):
                     head = 2 * pair + r
                     nc.scalar.activation(
                         out=e_rows[unit % E_BUFFERS][:, head, 0:keys],
-                        in_=held[("scores", unit, pair)][r][:, 0:keys],
+                        in_=held[("scores", unit, pair)][r],
                         func=ACT.Exp,
                         bias=held[("bias", unit, pair)][:, r : r + 1],
                         scale=SCALE,

@@ -30,7 +30,9 @@ PIECES = COLUMN_BLOCKS * PASSES
 SCALE = 1.0 / math.sqrt(HD)
 MASK_VALUE = -3.0e38
 E_BUFFERS = 2
-WEIGHTS_START = 13
+WEIGHTS_START = 12
+PROJECT_LAG = 5
+VECTOR_COLUMNS = 288
 
 FLOPS = 2 * (2 * HEADS * T * T * HD) + 2 * T * DIM * DIM
 
@@ -136,10 +138,9 @@ def tile_fusedselfattention_pa_kernel(tc, q, k, v, W_o, out):
             w_grouped = weights_stage.tile([P, N_TILE * PACK], BF16, align_bytes=64)
             grouped_runs = w_grouped[:].rearrange("p (m i t) -> p m t i", i=4, t=PACK)
             row_runs = rows.rearrange("p t (m i) -> p m t i", i=4)
-            if c < 2 or (c == 2 and n % 2 == 0):
-                nc.vector.tensor_copy(out=grouped_runs, in_=row_runs)
-            else:
-                nc.scalar.copy(out=grouped_runs, in_=row_runs)
+            runs = VECTOR_COLUMNS // 4
+            nc.vector.tensor_copy(out=grouped_runs[:, 0:runs], in_=row_runs[:, 0:runs])
+            nc.scalar.copy(out=grouped_runs[:, runs:], in_=row_runs[:, runs:])
             held[("w_grouped", piece)] = w_grouped
 
         def quantise_weights(piece):
@@ -344,51 +345,50 @@ def tile_fusedselfattention_pa_kernel(tc, q, k, v, W_o, out):
             def is_piece(piece):
                 return 0 <= piece < PIECES
 
-            for s in range(-3, WEIGHTS_START + PIECES + 7):
+            for s in range(-3, WEIGHTS_START + PIECES + PROJECT_LAG + 1):
                 w = s - WEIGHTS_START
                 if is_unit(s + 1):
                     scores_and_row_maxima(s + 1, 0)
                 if is_unit(s):
                     transpose_exponentials(s, 0)
-                    transpose_exponentials(s, 1)
                 if is_unit(s - 3):
                     copy_attention(s - 3)
+                if is_piece(w - PROJECT_LAG - 1) and (w - PROJECT_LAG - 1) % PASSES == PASSES - 1:
+                    store_column_block((w - PROJECT_LAG - 1) // PASSES)
                 if is_unit(s):
                     copy_exponentials(s, 0)
-                if is_piece(w - 7) and (w - 7) % PASSES == PASSES - 1:
-                    store_column_block((w - 7) // PASSES)
-                if is_piece(w - 4):
-                    project_piece(w - 4)
-                if s == 0:
-                    quantise_values()
+                    invert_row_sums(s)
+                if is_piece(w - PROJECT_LAG):
+                    project_piece(w - PROJECT_LAG)
                 if is_unit(s + 1):
                     exponent_biases(s + 1, 0)
                     scores_and_row_maxima(s + 1, 1)
+                if s == 0:
+                    quantise_values()
+                if is_unit(s):
+                    transpose_exponentials(s, 1)
+                    copy_exponentials(s, 1)
+                if is_piece(w):
+                    regroup_weights(w)
                 if is_unit(s - 1):
                     weighted_values(s - 1)
-                if is_unit(s):
-                    copy_exponentials(s, 1)
+                if is_unit(s + 1):
+                    exponent_biases(s + 1, 1)
+                if is_piece(w - 1):
+                    quantise_weights(w - 1)
                 if is_unit(s - 3):
                     quantise_attention(s - 3)
+                if is_unit(s + 1):
+                    exponentials(s + 1, 0)
                 if is_unit(s - 2):
                     transpose_attention(s - 2)
                 if is_unit(s + 1):
-                    exponentials(s + 1, 0)
-                if is_unit(s):
-                    invert_row_sums(s)
-                if is_unit(s + 1):
-                    exponent_biases(s + 1, 1)
+                    exponentials(s + 1, 1)
                 if is_unit(s - 1):
                     divide_by_row_sums(s - 1)
-                if is_unit(s):
-                    quantise_exponentials(s)
-                if is_piece(w):
-                    regroup_weights(w)
-                if is_unit(s + 1):
-                    exponentials(s + 1, 1)
                 if is_unit(s + 3):
                     if s + 3 < GROUPS:
                         transpose_keys(s + 3)
                     transpose_queries(s + 3)
-                if is_piece(w - 1):
-                    quantise_weights(w - 1)
+                if is_unit(s):
+                    quantise_exponentials(s)

@@ -25,14 +25,15 @@ PACK = 4
 K_PASS = P * PACK
 PASSES = DIM // K_PASS
 N_TILE = 512
-COLUMN_BLOCKS = DIM // N_TILE
-PIECES = COLUMN_BLOCKS * PASSES
+COLUMN_TILES = DIM // N_TILE
+COLUMN_BLOCKS = [(0, 512), (512, 512), (1024, 512), (1536, 256), (1792, 256)]
+PIECES = len(COLUMN_BLOCKS) * PASSES
 SCALE = 1.0 / math.sqrt(HD)
 MASK_VALUE = -3.0e38
 E_BUFFERS = 2
 WEIGHTS_START = 12
-PROJECT_LAG = 5
-VECTOR_COLUMNS = 288
+PROJECT_LAG = 4
+VECTOR_SHARE = 9
 
 FLOPS = 2 * (2 * HEADS * T * T * HD) + 2 * T * DIM * DIM
 
@@ -65,9 +66,9 @@ def tile_fusedselfattention_pa_kernel(tc, q, k, v, W_o, out):
         v_grouped = keep.tile([P, GROUPS * HD * PACK], BF16, align_bytes=64)
         v_codes = keep.tile([P, GROUPS * HD], U32, align_bytes=64)
         v_scales = keep.tile([P, GROUPS * HD], U8, align_bytes=64)
-        w_rows = [keep.tile([P, PASSES * PACK, N_TILE], BF16, name="w_rows%d" % n) for n in range(COLUMN_BLOCKS)]
-        w_codes = keep.tile([P, COLUMN_BLOCKS, PASSES, N_TILE], U32, align_bytes=64)
-        w_scales = keep.tile([P, COLUMN_BLOCKS, PASSES, N_TILE], U8, align_bytes=64)
+        w_rows = [keep.tile([P, PASSES * PACK, N_TILE], BF16, name="w_rows%d" % n) for n in range(COLUMN_TILES)]
+        w_codes = keep.tile([P, PASSES, DIM], U32, align_bytes=64)
+        w_scales = keep.tile([P, PASSES, DIM], U8, align_bytes=64)
         a_codes = keep.tile([P, BLOCKS, PASSES, P], U32, align_bytes=64)
         a_scales = keep.tile([P, BLOCKS, PASSES, P], U8, align_bytes=64)
         e_rows = [keep.tile([P, REP, T], BF16, name="e_rows%d" % b) for b in range(E_BUFFERS)]
@@ -101,7 +102,7 @@ def tile_fusedselfattention_pa_kernel(tc, q, k, v, W_o, out):
         )
         for unit in range(GROUPS, n_units):
             load_queries(unit)
-        for n in range(COLUMN_BLOCKS):
+        for n in range(COLUMN_TILES):
             load_weights(n)
 
         nc.vector.memset(warm[:], 0.0)
@@ -132,23 +133,30 @@ def tile_fusedselfattention_pa_kernel(tc, q, k, v, W_o, out):
         def quantise_values():
             nc.vector.quantize_mx(out=v_codes[:].bitcast(FP8X4), scales=v_scales[:], in_=v_grouped[:])
 
-        def regroup_weights(piece):
+        def regroup_weights_on_vector(piece):
             n, c = divmod(piece, PASSES)
-            rows = w_rows[n][:, c * PACK : (c + 1) * PACK, :]
+            first, width = COLUMN_BLOCKS[n]
+            column = first % N_TILE
+            rows = w_rows[first // N_TILE][:, c * PACK : (c + 1) * PACK, column : column + width]
             w_grouped = weights_stage.tile([P, N_TILE * PACK], BF16, align_bytes=64)
-            grouped_runs = w_grouped[:].rearrange("p (m i t) -> p m t i", i=4, t=PACK)
+            grouped_runs = w_grouped[:, 0 : width * PACK].rearrange("p (m i t) -> p m t i", i=4, t=PACK)
             row_runs = rows.rearrange("p t (m i) -> p m t i", i=4)
-            runs = VECTOR_COLUMNS // 4
+            runs = width // 4 * VECTOR_SHARE // 16
             nc.vector.tensor_copy(out=grouped_runs[:, 0:runs], in_=row_runs[:, 0:runs])
-            nc.scalar.copy(out=grouped_runs[:, runs:], in_=row_runs[:, runs:])
             held[("w_grouped", piece)] = w_grouped
+            held[("scalar_runs", piece)] = (grouped_runs[:, runs:], row_runs[:, runs:])
+
+        def regroup_weights_on_scalar(piece):
+            grouped_runs, row_runs = held[("scalar_runs", piece)]
+            nc.scalar.copy(out=grouped_runs, in_=row_runs)
 
         def quantise_weights(piece):
             n, c = divmod(piece, PASSES)
+            first, width = COLUMN_BLOCKS[n]
             nc.vector.quantize_mx(
-                out=w_codes[:, n, c, :].bitcast(FP8X4),
-                scales=w_scales[:, n, c, :],
-                in_=held[("w_grouped", piece)][:],
+                out=w_codes[:, c, first : first + width].bitcast(FP8X4),
+                scales=w_scales[:, c, first : first + width],
+                in_=held[("w_grouped", piece)][:, 0 : width * PACK],
             )
 
         with ExitStack() as psum:
@@ -310,11 +318,12 @@ def tile_fusedselfattention_pa_kernel(tc, q, k, v, W_o, out):
 
             def project_piece(piece):
                 n, c = divmod(piece, PASSES)
+                first, width = COLUMN_BLOCKS[n]
                 if c == 0:
                     banks = score_banks if n % 2 == 0 else other_banks
                     sums = []
                     for block in blocks_in_order:
-                        block_sum = banks.tile([P, N_TILE], F32, tag="bank")
+                        block_sum = banks.tile([P, width], F32, tag="bank")
                         sums.append(block_sum)
                     held[("sums", n)] = sums
                 for i, block in enumerate(blocks_in_order):
@@ -322,21 +331,22 @@ def tile_fusedselfattention_pa_kernel(tc, q, k, v, W_o, out):
                         out=held[("sums", n)][i][:],
                         lhsT=a_codes[:, block, c, :].bitcast(FP8X4),
                         lhsT_scale=a_scales[:, block, c, :],
-                        rhs=w_codes[:, n, c, :].bitcast(FP8X4),
-                        rhs_scale=w_scales[:, n, c, :],
+                        rhs=w_codes[:, c, first : first + width].bitcast(FP8X4),
+                        rhs_scale=w_scales[:, c, first : first + width],
                         start=(c == 0),
                         stop=(c == PASSES - 1),
                     )
 
             def store_column_block(n):
+                first, width = COLUMN_BLOCKS[n]
                 for i, block in enumerate(blocks_in_order):
-                    result = results.tile([P, N_TILE], F32)
+                    result = results.tile([P, width], F32)
                     if i < BLOCKS - 1:
                         nc.scalar.copy(out=result[:], in_=held[("sums", n)][i][:])
                     else:
                         nc.vector.tensor_copy(out=result[:], in_=held[("sums", n)][i][:])
                     nc.sync.dma_start(
-                        out=out[block * P : (block + 1) * P, n * N_TILE : (n + 1) * N_TILE], in_=result[:]
+                        out=out[block * P : (block + 1) * P, first : first + width], in_=result[:]
                     )
 
             def is_unit(unit):
@@ -347,48 +357,53 @@ def tile_fusedselfattention_pa_kernel(tc, q, k, v, W_o, out):
 
             for s in range(-3, WEIGHTS_START + PIECES + PROJECT_LAG + 1):
                 w = s - WEIGHTS_START
+                if is_unit(s - 3):
+                    copy_attention(s - 3)
                 if is_unit(s + 1):
                     scores_and_row_maxima(s + 1, 0)
                 if is_unit(s):
                     transpose_exponentials(s, 0)
-                if is_unit(s - 3):
-                    copy_attention(s - 3)
-                if is_piece(w - PROJECT_LAG - 1) and (w - PROJECT_LAG - 1) % PASSES == PASSES - 1:
-                    store_column_block((w - PROJECT_LAG - 1) // PASSES)
-                if is_unit(s):
-                    copy_exponentials(s, 0)
-                    invert_row_sums(s)
                 if is_piece(w - PROJECT_LAG):
                     project_piece(w - PROJECT_LAG)
                 if is_unit(s + 1):
-                    exponent_biases(s + 1, 0)
                     scores_and_row_maxima(s + 1, 1)
-                if s == 0:
-                    quantise_values()
-                if is_unit(s):
-                    transpose_exponentials(s, 1)
-                    copy_exponentials(s, 1)
                 if is_piece(w):
-                    regroup_weights(w)
-                if is_unit(s - 1):
-                    weighted_values(s - 1)
+                    regroup_weights_on_vector(w)
+                if is_unit(s):
+                    copy_exponentials(s, 0)
+                    transpose_exponentials(s, 1)
+                if is_unit(s + 1):
+                    exponent_biases(s + 1, 0)
+                if is_unit(s):
+                    copy_exponentials(s, 1)
+                if s + 1 == 0:
+                    exponentials(s + 1, 0)
                 if is_unit(s + 1):
                     exponent_biases(s + 1, 1)
-                if is_piece(w - 1):
-                    quantise_weights(w - 1)
-                if is_unit(s - 3):
-                    quantise_attention(s - 3)
-                if is_unit(s + 1):
-                    exponentials(s + 1, 0)
+                if is_unit(s - 1):
+                    weighted_values(s - 1)
                 if is_unit(s - 2):
                     transpose_attention(s - 2)
+                if is_unit(s - 3):
+                    quantise_attention(s - 3)
+                if is_unit(s + 1) and s + 1 > 0:
+                    exponentials(s + 1, 0)
                 if is_unit(s + 1):
                     exponentials(s + 1, 1)
                 if is_unit(s - 1):
                     divide_by_row_sums(s - 1)
+                if s == 0:
+                    quantise_values()
                 if is_unit(s + 3):
                     if s + 3 < GROUPS:
                         transpose_keys(s + 3)
                     transpose_queries(s + 3)
+                if is_piece(w):
+                    regroup_weights_on_scalar(w)
                 if is_unit(s):
+                    invert_row_sums(s)
                     quantise_exponentials(s)
+                if is_piece(w - 1):
+                    quantise_weights(w - 1)
+                if is_piece(w - PROJECT_LAG - 1) and (w - PROJECT_LAG - 1) % PASSES == PASSES - 1:
+                    store_column_block((w - PROJECT_LAG - 1) // PASSES)

@@ -75,8 +75,8 @@ def tile_fusedselfattention_pa_kernel(tc, q, k, v, W_o, out):
 
         def load_keys(group):
             nc.sync.dma_start(
-                out=k_rows[:, group * BLOCKS : (group + 1) * BLOCKS, :],
-                in_=k[group, :, :].rearrange("(b p) d -> p b d", p=P),
+                out=k_rows[:, group * BLOCKS : (group + 1) * BLOCKS, :].rearrange("p e d -> p (e d)"),
+                in_=k[group, :, :].rearrange("(p e) d -> p (e d)", e=BLOCKS),
             )
 
         def load_queries(unit):
@@ -167,7 +167,9 @@ def tile_fusedselfattention_pa_kernel(tc, q, k, v, W_o, out):
                 bank = other_banks.tile([P, BLOCKS, P], BF16, tag="bank")
                 for b in range(BLOCKS):
                     nc.tensor.transpose(bank[:, b, :], k_rows[:, group * BLOCKS + b, :], identity_bf16[:])
-                nc.scalar.copy(out=k_t[:, group, :], in_=bank[:].rearrange("p b j -> p (b j)"))
+                nc.scalar.copy(
+                    out=k_t[:, group, :].rearrange("d (p e) -> d p e", e=BLOCKS), in_=bank[:].rearrange("d e p -> d p e")
+                )
 
             def transpose_queries(unit):
                 block, group = units[unit]
@@ -254,13 +256,18 @@ def tile_fusedselfattention_pa_kernel(tc, q, k, v, W_o, out):
                     in_=held[("e_bank", unit, pair)][:].rearrange("p u x -> p x u"),
                 )
 
-            def quantise_exponentials(unit):
-                e_codes = stage.tile([P, REP * P], U32, align_bytes=64)
-                e_scales = stage.tile([P, REP * P], U8, align_bytes=64)
+            def quantise_exponentials(unit, pair):
+                if pair == 0:
+                    e_codes = stage.tile([P, REP * P], U32, align_bytes=64)
+                    e_scales = stage.tile([P, REP * P], U8, align_bytes=64)
+                    held[("e_codes", unit)] = (e_codes, e_scales)
+                e_codes, e_scales = held[("e_codes", unit)]
+                first, last = pair * 2 * P, (pair + 1) * 2 * P
                 nc.vector.quantize_mx(
-                    out=e_codes[:].bitcast(FP8X4), scales=e_scales[:], in_=held[("e_grouped", unit)][:]
+                    out=e_codes[:, first:last].bitcast(FP8X4),
+                    scales=e_scales[:, first:last],
+                    in_=held[("e_grouped", unit)][:, first * PACK : last * PACK],
                 )
-                held[("e_codes", unit)] = (e_codes, e_scales)
 
             def weighted_values(unit):
                 block, group = units[unit]
@@ -392,6 +399,8 @@ def tile_fusedselfattention_pa_kernel(tc, q, k, v, W_o, out):
                     exponentials(s + 1, 1)
                 if is_unit(s - 1):
                     divide_by_row_sums(s - 1)
+                if is_unit(s):
+                    quantise_exponentials(s, 0)
                 if s == 0:
                     quantise_values()
                 if is_unit(s + 3):
@@ -402,7 +411,7 @@ def tile_fusedselfattention_pa_kernel(tc, q, k, v, W_o, out):
                     regroup_weights_on_scalar(w)
                 if is_unit(s):
                     invert_row_sums(s)
-                    quantise_exponentials(s)
+                    quantise_exponentials(s, 1)
                 if is_piece(w - 1):
                     quantise_weights(w - 1)
                 if is_piece(w - PROJECT_LAG - 1) and (w - PROJECT_LAG - 1) % PASSES == PASSES - 1:

@@ -30,6 +30,7 @@ COLUMN_BLOCKS = [(0, 512), (512, 512), (1024, 512), (1536, 256), (1792, 256)]
 PIECES = len(COLUMN_BLOCKS) * PASSES
 SCALE = 1.0 / math.sqrt(HD)
 MASK_VALUE = -3.0e38
+WARM_UP = 3
 E_BUFFERS = 2
 WEIGHTS_START = 12
 PROJECT_LAG = 4
@@ -58,6 +59,7 @@ def tile_fusedselfattention_pa_kernel(tc, q, k, v, W_o, out):
         causal_f32 = keep.tile([P, P], F32)
         causal_mask = keep.tile([P, P], BF16)
         warm = keep.tile([P, 1], F32)
+        zeros = keep.tile([P, T], BF16)
         k_rows = keep.tile([P, GROUPS * BLOCKS, HD], BF16)
         k_t = keep.tile([P, GROUPS, T], BF16)
         q_rows = [keep.tile([P, HEADS, HD], BF16, name="q_rows%d" % b) for b in range(BLOCKS)]
@@ -106,6 +108,7 @@ def tile_fusedselfattention_pa_kernel(tc, q, k, v, W_o, out):
             load_weights(n)
 
         nc.vector.memset(warm[:], 0.0)
+        nc.vector.memset(zeros[:], 0.0)
         nc.scalar.activation(out=warm[:], in_=warm[:], func=ACT.Exp)
         make_identity(nc, identity_bf16[:])
         make_identity(nc, identity_f32[:])
@@ -162,6 +165,10 @@ def tile_fusedselfattention_pa_kernel(tc, q, k, v, W_o, out):
         with ExitStack() as psum:
             score_banks = psum.enter_context(tc.psum_pool(name="score_banks", bufs=4))
             other_banks = psum.enter_context(tc.psum_pool(name="other_banks", bufs=4))
+
+            for i in range(WARM_UP):
+                bank = score_banks.tile([P, T], F32, tag="bank")
+                nc.tensor.matmul(bank[:], lhsT=zeros[:, 0:P], rhs=zeros[:], start=True, stop=True)
 
             def transpose_keys(group):
                 bank = other_banks.tile([P, BLOCKS, P], BF16, tag="bank")

import math
from contextlib import ExitStack

import concourse.mybir as mybir
from concourse.masks import make_identity

F32 = mybir.dt.float32
BF16 = mybir.dt.bfloat16
U32 = mybir.dt.uint32
U8 = mybir.dt.uint8
FP8X4 = mybir.dt.float8_e4m3fn_x4
ALU = mybir.AluOpType
ACT = mybir.ActivationFunctionType
AXIS = mybir.AxisListType

P = 128
T = 512
HEADS = 16
GROUPS = 4
REP = HEADS // GROUPS
HD = 128
DIM = HEADS * HD
BLOCKS = T // P
PACK = 4
K_PASS = P * PACK
PASSES = DIM // K_PASS
N_TILE = 512
COLUMN_TILES = DIM // N_TILE
COLUMN_BLOCKS = [(0, 512), (512, 512), (1024, 512), (1536, 256), (1792, 256)]
PIECES = len(COLUMN_BLOCKS) * PASSES
SCALE = 1.0 / math.sqrt(HD)
MASK_VALUE = -3.0e38
WARM_UP = 3
E_BUFFERS = 2
WEIGHTS_START = 12
PROJECT_LAG = 4
VECTOR_SHARE = 9

FLOPS = 2 * (2 * HEADS * T * T * HD) + 2 * T * DIM * DIM


def tile_fusedselfattention_pa_kernel(tc, q, k, v, W_o, out):
    nc = tc.nc
    units = [(block, group) for block in reversed(range(BLOCKS)) for group in range(GROUPS)]
    n_units = len(units)
    blocks_in_order = [units[i * GROUPS][0] for i in range(BLOCKS)]
    held = {}

    with ExitStack() as sbuf:
        sbuf.enter_context(tc.manual_schedule())
        keep = sbuf.enter_context(tc.tile_pool(name="keep", bufs=1))
        stats = sbuf.enter_context(tc.tile_pool(name="stats", bufs=3))
        stage = sbuf.enter_context(tc.tile_pool(name="stage", bufs=2))
        weights_stage = sbuf.enter_context(tc.tile_pool(name="weights_stage", bufs=4))
        results = sbuf.enter_context(tc.tile_pool(name="results", bufs=2 * BLOCKS))

        identity_bf16 = keep.tile([P, P], BF16)
        identity_f32 = keep.tile([P, P], F32)
        causal_f32 = keep.tile([P, P], F32)
        causal_mask = keep.tile([P, P], BF16)
        warm = keep.tile([P, 1], F32)
        zeros = keep.tile([P, T], BF16)
        k_rows = keep.tile([P, GROUPS * BLOCKS, HD], BF16)
        k_t = keep.tile([P, GROUPS, T], BF16)
        q_rows = [keep.tile([P, HEADS, HD], BF16, name="q_rows%d" % b) for b in range(BLOCKS)]
        q_t = [keep.tile([P, HEADS, P], BF16, name="q_t%d" % b) for b in range(BLOCKS)]
        v_rows = keep.tile([P, GROUPS * PACK, HD], BF16)
        v_grouped = keep.tile([P, GROUPS * HD * PACK], BF16, align_bytes=64)
        v_codes = keep.tile([P, GROUPS * HD], U32, align_bytes=64)
        v_scales = keep.tile([P, GROUPS * HD], U8, align_bytes=64)
        w_rows = [keep.tile([P, PASSES * PACK, N_TILE], BF16, name="w_rows%d" % n) for n in range(COLUMN_TILES)]
        w_codes = keep.tile([P, PASSES, DIM], U32, align_bytes=64)
        w_scales = keep.tile([P, PASSES, DIM], U8, align_bytes=64)
        a_codes = keep.tile([P, BLOCKS, PASSES, P], U32, align_bytes=64)
        a_scales = keep.tile([P, BLOCKS, PASSES, P], U8, align_bytes=64)
        e_rows = [keep.tile([P, REP, T], BF16, name="e_rows%d" % b) for b in range(E_BUFFERS)]

        def load_keys(group):
            nc.sync.dma_start(
                out=k_rows[:, group * BLOCKS : (group + 1) * BLOCKS, :].rearrange("p e d -> p (e d)"),
                in_=k[group, :, :].rearrange("(p e) d -> p (e d)", e=BLOCKS),
            )

        def load_queries(unit):
            block, group = units[unit]
            heads = slice(group * REP, (group + 1) * REP)
            nc.sync.dma_start(
                out=q_rows[block][:, heads, :],
                in_=q[heads, block * P : (block + 1) * P, :].rearrange("h p d -> p h d"),
            )

        def load_weights(n):
            columns = W_o[:, n * N_TILE : (n + 1) * N_TILE].rearrange("(cu p e) n -> p cu e n", p=P, e=2)
            rows = w_rows[n][:].rearrange("p (cu e) n -> p cu e n", e=2)
            for e in range(2):
                nc.sync.dma_start(out=rows[:, :, e, :], in_=columns[:, :, e, :])

        for group in range(GROUPS):
            load_keys(group)
            load_queries(group)
        nc.sync.dma_start(
            out=v_rows[:].rearrange("p (gu e) d -> p gu (e d)", e=2),
            in_=v.rearrange("g (u p e) d -> p (g u) (e d)", u=2, p=P, e=2),
        )
        for unit in range(GROUPS, n_units):
            load_queries(unit)
        for n in range(COLUMN_TILES):
            load_weights(n)

        nc.vector.memset(warm[:], 0.0)
        nc.vector.memset(zeros[:], 0.0)
        nc.scalar.activation(out=warm[:], in_=warm[:], func=ACT.Exp)
        make_identity(nc, identity_bf16[:])
        make_identity(nc, identity_f32[:])
        nc.gpsimd.memset(causal_f32[:], 0.0)
        nc.gpsimd.affine_select(
            out=causal_f32[:],
            in_=causal_f32[:],
            pattern=[[-1, P]],
            compare_op=ALU.is_ge,
            fill=MASK_VALUE,
            base=0,
            channel_multiplier=1,
        )
        nc.vector.tensor_copy(out=causal_mask[:], in_=causal_f32[:])

        nc.gpsimd.tensor_scalar(
            out=v_grouped[:].rearrange("p (g d t) -> p g d t", g=GROUPS, t=PACK),
            in0=v_rows[:].rearrange("p (g t) d -> p g d t", t=PACK),
            scalar1=1.0,
            scalar2=0.0,
            op0=ALU.mult,
            op1=ALU.add,
        )

        def quantise_values():
            nc.vector.quantize_mx(out=v_codes[:].bitcast(FP8X4), scales=v_scales[:], in_=v_grouped[:])

        def regroup_weights_on_vector(piece):
            n, c = divmod(piece, PASSES)
            first, width = COLUMN_BLOCKS[n]
            column = first % N_TILE
            rows = w_rows[first // N_TILE][:, c * PACK : (c + 1) * PACK, column : column + width]
            w_grouped = weights_stage.tile([P, N_TILE * PACK], BF16, align_bytes=64)
            grouped_runs = w_grouped[:, 0 : width * PACK].rearrange("p (m i t) -> p m t i", i=4, t=PACK)
            row_runs = rows.rearrange("p t (m i) -> p m t i", i=4)
            runs = width // 4 * VECTOR_SHARE // 16
            nc.vector.tensor_copy(out=grouped_runs[:, 0:runs], in_=row_runs[:, 0:runs])
            held[("w_grouped", piece)] = w_grouped
            held[("scalar_runs", piece)] = (grouped_runs[:, runs:], row_runs[:, runs:])

        def regroup_weights_on_scalar(piece):
            grouped_runs, row_runs = held[("scalar_runs", piece)]
            nc.scalar.copy(out=grouped_runs, in_=row_runs)

        def quantise_weights(piece):
            n, c = divmod(piece, PASSES)
            first, width = COLUMN_BLOCKS[n]
            nc.vector.quantize_mx(
                out=w_codes[:, c, first : first + width].bitcast(FP8X4),
                scales=w_scales[:, c, first : first + width],
                in_=held[("w_grouped", piece)][:, 0 : width * PACK],
            )

        with ExitStack() as psum:
            score_banks = psum.enter_context(tc.psum_pool(name="score_banks", bufs=4))
            other_banks = psum.enter_context(tc.psum_pool(name="other_banks", bufs=4))

            for i in range(WARM_UP):
                bank = score_banks.tile([P, T], F32, tag="bank")
                nc.tensor.matmul(bank[:], lhsT=zeros[:, 0:P], rhs=zeros[:], start=True, stop=True)

            def transpose_keys(group):
                bank = other_banks.tile([P, BLOCKS, P], BF16, tag="bank")
                for b in range(BLOCKS):
                    nc.tensor.transpose(bank[:, b, :], k_rows[:, group * BLOCKS + b, :], identity_bf16[:])
                nc.scalar.copy(
                    out=k_t[:, group, :].rearrange("d (p e) -> d p e", e=BLOCKS), in_=bank[:].rearrange("d e p -> d p e")
                )

            def transpose_queries(unit):
                block, group = units[unit]
                bank = other_banks.tile([P, REP, P], BF16, tag="bank")
                for r in range(REP):
                    nc.tensor.transpose(bank[:, r, :], q_rows[block][:, group * REP + r, :], identity_bf16[:])
                nc.vector.tensor_copy(out=q_t[block][:, group * REP : (group + 1) * REP, :], in_=bank[:])

            def scores_and_row_maxima(unit, pair):
                block, group = units[unit]
                keys = (block + 1) * P
                per_bank = 1 if block > 1 else 2
                diagonal = slice(block * P, keys)
                if pair == 0 and block < BLOCKS - 1 and group < E_BUFFERS:
                    nc.gpsimd.memset(e_rows[unit % E_BUFFERS][:, :, keys : keys + P], 0.0)
                row_max = stats.tile([P, 2], F32)
                banks = []
                for r in range(2):
                    queries = q_t[block][:, group * REP + 2 * pair + r, :]
                    if r % per_bank == 0:
                        bank = score_banks.tile([P, per_bank, T // per_bank], F32, tag="bank")
                    scores = bank[:, r % per_bank, 0:keys]
                    if block > 0:
                        nc.tensor.matmul(
                            scores[:, 0 : block * P],
                            lhsT=queries,
                            rhs=k_t[:, group, 0 : block * P],
                            start=True,
                            stop=True,
                        )
                    nc.tensor.matmul(
                        scores[:, diagonal], lhsT=queries, rhs=k_t[:, group, diagonal], start=True, stop=False
                    )
                    nc.tensor.matmul(
                        scores[:, diagonal], lhsT=identity_bf16[:], rhs=causal_mask[:], start=False, stop=True
                    )
                    if r % per_bank == per_bank - 1:
                        nc.vector.tensor_reduce(
                            out=row_max[:, r + 1 - per_bank : r + 1], in_=bank[:, :, 0:keys], axis=AXIS.X, op=ALU.max
                        )
                    banks.append(scores)
                held[("scores", unit, pair)] = banks
                held[("row_max", unit, pair)] = row_max

            def exponent_biases(unit, pair):
                bias = stats.tile([P, 2], F32)
                nc.scalar.activation(out=bias[:], in_=held[("row_max", unit, pair)][:], func=ACT.Copy, scale=-SCALE)
                held[("bias", unit, pair)] = bias

            def exponentials(unit, pair):
                block, group = units[unit]
                keys = (block + 1) * P
                if pair == 0:
                    row_sum = stats.tile([P, REP], F32)
                    held[("row_sum", unit)] = row_sum
                for r in range(2):
                    head = 2 * pair + r
                    nc.scalar.activation(
                        out=e_rows[unit % E_BUFFERS][:, head, 0:keys],
                        in_=held[("scores", unit, pair)][r],
                        func=ACT.Exp,
                        bias=held[("bias", unit, pair)][:, r : r + 1],
                        scale=SCALE,
                        accum_out=held[("row_sum", unit)][:, head : head + 1],
                    )

            def transpose_exponentials(unit, pair):
                bank = other_banks.tile([P, 2, 2 * P], F32, tag="bank")
                for r in range(2):
                    words = e_rows[unit % E_BUFFERS][:, 2 * pair + r, :].bitcast(F32)
                    for u in range(2):
                        nc.tensor.transpose(
                            bank[:, u, r * P : (r + 1) * P], words[:, u * P : (u + 1) * P], identity_f32[:]
                        )
                held[("e_bank", unit, pair)] = bank

            def copy_exponentials(unit, pair):
                if pair == 0:
                    e_grouped = stage.tile([P, REP * P * PACK], BF16, align_bytes=64)
                    held[("e_grouped", unit)] = e_grouped
                grouped_words = held[("e_grouped", unit)][:].bitcast(F32).rearrange("p (x u) -> p x u", u=2)
                nc.scalar.copy(
                    out=grouped_words[:, pair * 2 * P : (pair + 1) * 2 * P, :],
                    in_=held[("e_bank", unit, pair)][:].rearrange("p u x -> p x u"),
                )

            def quantise_exponentials(unit, pair):
                if pair == 0:
                    e_codes = stage.tile([P, REP * P], U32, align_bytes=64)
                    e_scales = stage.tile([P, REP * P], U8, align_bytes=64)
                    held[("e_codes", unit)] = (e_codes, e_scales)
                e_codes, e_scales = held[("e_codes", unit)]
                first, last = pair * 2 * P, (pair + 1) * 2 * P
                nc.vector.quantize_mx(
                    out=e_codes[:, first:last].bitcast(FP8X4),
                    scales=e_scales[:, first:last],
                    in_=held[("e_grouped", unit)][:, first * PACK : last * PACK],
                )

            def weighted_values(unit):
                block, group = units[unit]
                e_codes, e_scales = held[("e_codes", unit)]
                o_bank = other_banks.tile([P, REP, HD], F32, tag="bank")
                for r in range(REP):
                    nc.tensor.matmul_mx(
                        out=o_bank[:, r, :],
                        lhsT=e_codes[:, r * P : (r + 1) * P].bitcast(FP8X4),
                        lhsT_scale=e_scales[:, r * P : (r + 1) * P],
                        rhs=v_codes[:, group * HD : (group + 1) * HD].bitcast(FP8X4),
                        rhs_scale=v_scales[:, group * HD : (group + 1) * HD],
                        start=True,
                        stop=True,
                    )
                held[("o_bank", unit)] = o_bank

            def invert_row_sums(unit):
                inverse_sum = stats.tile([P, REP], F32)
                nc.vector.reciprocal(out=inverse_sum[:], in_=held[("row_sum", unit)][:])
                held[("inverse_sum", unit)] = inverse_sum

            def divide_by_row_sums(unit):
                a_rows = stage.tile([P, REP * HD], BF16)
                nc.vector.tensor_tensor(
                    out=a_rows[:].rearrange("p (r d) -> p r d", r=REP),
                    in0=held[("o_bank", unit)][:],
                    in1=held[("inverse_sum", unit)][:].unsqueeze(2).to_broadcast([P, REP, HD]),
                    op=ALU.mult,
                )
                held[("a_rows", unit)] = a_rows

            def transpose_attention(unit):
                words = held[("a_rows", unit)][:].bitcast(F32)
                bank = other_banks.tile([P, 2, P], F32, tag="bank")
                for u in range(2):
                    nc.tensor.transpose(bank[:, u, :], words[:, u * P : (u + 1) * P], identity_f32[:])
                held[("a_bank", unit)] = bank

            def copy_attention(unit):
                a_grouped = stage.tile([P, P * PACK], BF16, align_bytes=64)
                nc.scalar.copy(
                    out=a_grouped[:].bitcast(F32).rearrange("p (i u) -> p i u", u=2),
                    in_=held[("a_bank", unit)][:].rearrange("p u i -> p i u"),
                )
                held[("a_grouped", unit)] = a_grouped

            def quantise_attention(unit):
                block, group = units[unit]
                nc.vector.quantize_mx(
                    out=a_codes[:, block, group, :].bitcast(FP8X4),
                    scales=a_scales[:, block, group, :],
                    in_=held[("a_grouped", unit)][:],
                )

            def project_piece(piece):
                n, c = divmod(piece, PASSES)
                first, width = COLUMN_BLOCKS[n]
                if c == 0:
                    banks = score_banks if n % 2 == 0 else other_banks
                    sums = []
                    for block in blocks_in_order:
                        block_sum = banks.tile([P, width], F32, tag="bank")
                        sums.append(block_sum)
                    held[("sums", n)] = sums
                for i, block in enumerate(blocks_in_order):
                    nc.tensor.matmul_mx(
                        out=held[("sums", n)][i][:],
                        lhsT=a_codes[:, block, c, :].bitcast(FP8X4),
                        lhsT_scale=a_scales[:, block, c, :],
                        rhs=w_codes[:, c, first : first + width].bitcast(FP8X4),
                        rhs_scale=w_scales[:, c, first : first + width],
                        start=(c == 0),
                        stop=(c == PASSES - 1),
                    )

            def store_column_block(n):
                first, width = COLUMN_BLOCKS[n]
                for i, block in enumerate(blocks_in_order):
                    result = results.tile([P, width], F32)
                    if i < BLOCKS - 1:
                        nc.scalar.copy(out=result[:], in_=held[("sums", n)][i][:])
                    else:
                        nc.vector.tensor_copy(out=result[:], in_=held[("sums", n)][i][:])
                    nc.sync.dma_start(
                        out=out[block * P : (block + 1) * P, first : first + width], in_=result[:]
                    )

            def is_unit(unit):
                return 0 <= unit < n_units

            def is_piece(piece):
                return 0 <= piece < PIECES

            for s in range(-3, WEIGHTS_START + PIECES + PROJECT_LAG + 1):
                w = s - WEIGHTS_START
                if is_unit(s - 3):
                    copy_attention(s - 3)
                if is_unit(s + 1):
                    scores_and_row_maxima(s + 1, 0)
                if is_unit(s):
                    transpose_exponentials(s, 0)
                if is_piece(w - PROJECT_LAG):
                    project_piece(w - PROJECT_LAG)
                if is_unit(s + 1):
                    scores_and_row_maxima(s + 1, 1)
                if is_piece(w):
                    regroup_weights_on_vector(w)
                if is_unit(s):
                    copy_exponentials(s, 0)
                    transpose_exponentials(s, 1)
                if is_unit(s + 1):
                    exponent_biases(s + 1, 0)
                if is_unit(s):
                    copy_exponentials(s, 1)
                if s + 1 == 0:
                    exponentials(s + 1, 0)
                if is_unit(s + 1):
                    exponent_biases(s + 1, 1)
                if is_unit(s - 1):
                    weighted_values(s - 1)
                if is_unit(s - 2):
                    transpose_attention(s - 2)
                if is_unit(s - 3):
                    quantise_attention(s - 3)
                if is_unit(s + 1) and s + 1 > 0:
                    exponentials(s + 1, 0)
                if is_unit(s + 1):
                    exponentials(s + 1, 1)
                if is_unit(s - 1):
                    divide_by_row_sums(s - 1)
                if is_unit(s):
                    quantise_exponentials(s, 0)
                if s == 0:
                    quantise_values()
                if is_unit(s + 3):
                    if s + 3 < GROUPS:
                        transpose_keys(s + 3)
                    transpose_queries(s + 3)
                if is_piece(w):
                    regroup_weights_on_scalar(w)
                if is_unit(s):
                    invert_row_sums(s)
                    quantise_exponentials(s, 1)
                if is_piece(w - 1):
                    quantise_weights(w - 1)
                if is_piece(w - PROJECT_LAG - 1) and (w - PROJECT_LAG - 1) % PASSES == PASSES - 1:
                    store_column_block((w - PROJECT_LAG - 1) // PASSES)
